import numpy as np
import ml_dtypes


def mxq(x, axis, fmt="e4m3"):
    dtype, down = {"e4m3": (ml_dtypes.float8_e4m3fn, 7), "e5m2": (ml_dtypes.float8_e5m2, 14)}[fmt]
    v = np.moveaxis(np.asarray(x, np.float32).astype(ml_dtypes.bfloat16).astype(np.float64), axis, -1)
    blocks = v.reshape(v.shape[:-1] + (-1, 32))
    amax = np.abs(blocks).max(-1, keepdims=True)
    byte = np.maximum(np.where(amax > 0, np.frexp(amax)[1] - 1 + 127, 0) - down, 1)
    scale = np.exp2(byte - 127.0)
    codes = (blocks / scale).astype(np.float32).astype(dtype).astype(np.float64)
    return np.moveaxis((codes * scale).reshape(v.shape), -1, axis)


WIDE = False


def mx_kscale(k):
    if not WIDE:
        return np.ones(k)
    levels = np.array([10, -10, 5, -5, 0])
    if k % 512:
        return np.exp2(np.random.permutation(np.resize(levels, k // 32))).repeat(32)
    a = np.empty((k // 512, 16))
    for p in range(k // 512):
        a[p, :8] = np.random.permutation(np.resize(levels, 8))
        for g in range(8):
            far = levels[np.abs(levels - a[p, g]) >= 10]
            a[p, g + 8] = far[np.random.randint(len(far))]
    return np.exp2(a.ravel()).repeat(32)


BF16 = ml_dtypes.bfloat16


def bf(x):
    return np.asarray(x, np.float32).astype(BF16)


def f64(x):
    return np.asarray(x).astype(np.float64)


N, F, M, E, H, G, C = 2048, 1024, 512, 512, 256, 128, 10


def draw_adj():
    p = np.random.standard_normal(N)
    return np.exp(1.5 * np.random.standard_normal((N, N)) + 0.5 * p[:, None] + 0.5 * p[None, :]) * 0.3 / N


def setup_inputs():
    s = mx_kscale(N)
    c = s / np.exp2(np.round(np.log2(s.mean())))
    return {"h_gcn1": bf(np.maximum(np.random.standard_normal((N, H)), 0.0) / c[:, None]),
            "adj": bf(draw_adj() * c),
            "gcn2_w": bf(np.random.standard_normal((H, G)) * 1.5 / np.sqrt(H)),
            "gcn2_b": bf(np.random.standard_normal(G) * 0.1)}


def reference(h_gcn1, adj, gcn2_w, gcn2_b):
    a = f64(adj)
    deg = a.sum(axis=1)
    dis = deg ** -0.5
    xw = f64(h_gcn1) @ f64(gcn2_w)
    y = dis[:, None] * xw
    agg = mxq(a, 1, "e4m3") @ mxq(y, 0, "e4m3")
    return np.maximum(dis[:, None] * agg + f64(gcn2_b), 0.0)

@@ -1,0 +1,208 @@
+from contextlib import ExitStack
+
+import concourse.mybir as mybir
+from concourse.masks import make_identity
+
+F32 = mybir.dt.float32
+BF16 = mybir.dt.bfloat16
+U32 = mybir.dt.uint32
+U8 = mybir.dt.uint8
+FP8X4 = mybir.dt.float8_e4m3fn_x4
+ALU = mybir.AluOpType
+ACT = mybir.ActivationFunctionType
+
+P = 128
+N_NODES = 2048
+H_IN = 256
+G_OUT = 128
+TILES = 16
+PASSES = 4
+HALF = N_NODES // 2
+
+FLOPS = 2 * N_NODES * N_NODES * G_OUT + 2 * N_NODES * H_IN * G_OUT
+
+SCALAR_DEGREES = (2, 6, 10)
+H_AFTER = 3
+
+
+def tile_gcnclassifer_pb_kernel(tc, h_gcn1, adj, gcn2_w, gcn2_b, out):
+    nc = tc.nc
+    with ExitStack() as ctx:
+        keep = ctx.enter_context(tc.tile_pool(name="keep", bufs=1))
+        stage = ctx.enter_context(tc.tile_pool(name="stage", bufs=8))
+        junk = ctx.enter_context(tc.tile_pool(name="junk", bufs=2))
+        small = ctx.enter_context(tc.tile_pool(name="small", bufs=4))
+        ps_t = ctx.enter_context(tc.psum_pool(name="ps_t", bufs=7))
+        ps_x = ctx.enter_context(tc.psum_pool(name="ps_x", bufs=1))
+
+        one = keep.tile([P, 1], F32)
+        nc.vector.memset(one[:], 1.0)
+        warm = keep.tile([P, 1], F32)
+        nc.scalar.sqrt(out=warm[:], in_=one[:])
+        ident = keep.tile([P, P], F32)
+        make_identity(nc, ident[:])
+
+        a_sb = keep.tile([P, TILES, N_NODES], BF16)
+        w_sb = keep.tile([P, 2, G_OUT], BF16)
+        h_sb = keep.tile([P, TILES, H_IN], BF16)
+        bias = keep.tile([P, G_OUT], BF16)
+
+        adj_v = adj.rearrange("(b p e) j -> p b e j", p=P, e=4)
+        for r in range(TILES):
+            if r == 0:
+                nc.sync.dma_start(out=a_sb[:, r, 0:HALF], in_=adj_v[:, 0, 0, 0:HALF])
+                nc.sync.dma_start(out=a_sb[:, r, HALF:N_NODES], in_=adj_v[:, 0, 0, HALF:N_NODES])
+            else:
+                nc.sync.dma_start(out=a_sb[:, r, :], in_=adj_v[:, r // 4, r % 4, :])
+            if r == H_AFTER:
+                nc.sync.dma_start(out=w_sb[:], in_=gcn2_w.rearrange("(q k) g -> q k g", k=2))
+                nc.sync.dma_start(
+                    out=h_sb[:].rearrange("p (b e) k -> p b (e k)", e=4),
+                    in_=h_gcn1.rearrange("(b p e) k -> p b (e k)", p=P, e=4),
+                )
+
+        nc.sync.dma_start(out=bias[:], in_=gcn2_b.partition_broadcast(P))
+
+        deg = keep.tile([P, TILES, 8], F32)
+        dis = keep.tile([P, TILES], F32)
+        codes = keep.tile([P, TILES, 512], U32, align_bytes=64)
+        scales = keep.tile([P, TILES, 512], U8, align_bytes=64)
+        h_t = keep.tile([P, TILES, P], F32)
+        y_g = keep.tile([P, PASSES, G_OUT, 4], BF16, align_bytes=64)
+        y_codes = keep.tile([P, PASSES, G_OUT], U32, align_bytes=64)
+        y_scales = keep.tile([P, PASSES, G_OUT], U8, align_bytes=64)
+        z_sb = keep.tile([P, TILES, G_OUT], F32)
+        o_sb = keep.tile([P, TILES, G_OUT], F32)
+        out_v = out.rearrange("(b p e) g -> p b (e g)", p=P, e=4)
+        grouped = {}
+
+        def degree(r):
+            acc = deg[:, r, 0:1]
+            if r in SCALAR_DEGREES:
+                js = junk.tile([P, N_NODES], BF16)
+                nc.scalar.activation(out=js[:], in_=a_sb[:, r, :], func=ACT.Copy, accum_out=acc)
+            else:
+                jv = junk.tile([P, HALF], F32)
+                nc.vector.scalar_tensor_tensor(
+                    out=jv[:],
+                    in0=a_sb[:, r, 0:HALF],
+                    scalar=1.0,
+                    in1=a_sb[:, r, HALF:N_NODES],
+                    op0=ALU.mult,
+                    op1=ALU.add,
+                    accum_out=acc,
+                )
+
+        def flip(r):
+            words = a_sb[:, r, :].bitcast(F32)
+            g_t = stage.tile([P, 4 * 512], BF16, align_bytes=64, name="g_t")
+            grouped[r] = g_t
+            g_w = g_t[:].bitcast(F32).rearrange("p (c i u) -> p c i u", c=4, u=2)
+            for half in range(2):
+                xt = ps_t.tile([P, 2, 2, P], F32, name="xt")
+                for cc in range(2):
+                    for u in range(2):
+                        first = 256 * (2 * half + cc)
+                        nc.tensor.transpose(xt[:, cc, u, :], words[:, first + u : first + 256 : 2], ident[:])
+                nc.scalar.copy(
+                    out=g_w[:, 2 * half : 2 * half + 2, :, :], in_=xt[:].rearrange("p c u i -> p c i u")
+                )
+
+        def quantise(r):
+            nc.vector.quantize_mx(
+                out=codes[:, r, :].bitcast(FP8X4), scales=scales[:, r, :], in_=grouped[r][:]
+            )
+
+        def flip_h():
+            h_w = h_sb[:].bitcast(F32)
+            for q in range(PASSES):
+                ht = ps_t.tile([P, 4, P], F32, name="xt")
+                for t in range(4):
+                    nc.tensor.transpose(ht[:, t, :], h_w[:, 4 * q + t, :], ident[:])
+                nc.scalar.copy(out=h_t[:, 4 * q : 4 * q + 4, :], in_=ht[:])
+
+        def make_y(c):
+            rt = small.tile([P, 4], F32, name="rt")
+            nc.scalar.sqrt(out=rt[:], in_=deg[:, 4 * c : 4 * c + 4, 0])
+            nc.vector.reciprocal(out=dis[:, 4 * c : 4 * c + 4], in_=rt[:])
+            h_b = h_t[:].bitcast(BF16).rearrange("p r (j k) -> p r j k", k=2)
+            xw = ps_x.tile([P, 4, G_OUT], F32, name="xw")
+            for t in range(4):
+                for k in range(2):
+                    nc.tensor.matmul(
+                        out=xw[:, t, :],
+                        lhsT=h_b[:, 4 * c + t, :, k],
+                        rhs=w_sb[:, k, :],
+                        start=(k == 0),
+                        stop=(k == 1),
+                    )
+            nc.vector.tensor_tensor(
+                out=y_g[:, c, :, :],
+                in0=xw[:].rearrange("p t g -> p g t"),
+                in1=dis[:, 4 * c : 4 * c + 4].unsqueeze(1).to_broadcast([P, G_OUT, 4]),
+                op=ALU.mult,
+            )
+            nc.vector.quantize_mx(
+                out=y_codes[:, c, :].bitcast(FP8X4),
+                scales=y_scales[:, c, :],
+                in_=y_g[:, c, :, :].rearrange("p g t -> p (g t)"),
+            )
+
+        acc = {}
+
+        issued = set()
+
+        def passes(m, c):
+            if m not in acc:
+                acc_ps = ps_t.tile([P, 4, G_OUT], F32, name="xt")
+                acc[m] = acc_ps
+            for t in range(4):
+                r = 4 * m + t
+                nc.tensor.matmul_mx(
+                    out=acc[m][:, t, :],
+                    lhsT=codes[:, r, 128 * c : 128 * c + 128].bitcast(FP8X4),
+                    lhsT_scale=scales[:, r, 128 * c : 128 * c + 128],
+                    rhs=y_codes[:, c, :].bitcast(FP8X4),
+                    rhs_scale=y_scales[:, c, :],
+                    start=(c == 0 and t == 0),
+                    stop=(c == PASSES - 1 and t == 3),
+                )
+
+        def epilogue(m):
+            for t in range(4):
+                r = 4 * m + t
+                nc.vector.scalar_tensor_tensor(
+                    out=z_sb[:, r, :],
+                    in0=acc[m][:, t, :],
+                    scalar=dis[:, r : r + 1],
+                    in1=bias[:],
+                    op0=ALU.mult,
+                    op1=ALU.add,
+                )
+            nc.scalar.activation(
+                out=o_sb[:, 4 * m : 4 * m + 4, :], in_=z_sb[:, 4 * m : 4 * m + 4, :], func=ACT.Relu
+            )
+            nc.sync.dma_start(
+                out=out_v[:, m, :],
+                in_=o_sb[:, 4 * m : 4 * m + 4, :].rearrange("p e g -> p (e g)"),
+            )
+
+        for c in range(PASSES + 1):
+            if c < PASSES:
+                for r in range(4 * c, 4 * c + 4):
+                    degree(r)
+                    flip(r)
+                    if r == H_AFTER:
+                        flip_h()
+                make_y(c)
+            if c > 0:
+                for r in range(4 * c - 4, 4 * c):
+                    quantise(r)
+                known = min(c, PASSES - 1) + 1
+                for m in range(c):
+                    for k in range(known):
+                        if (m, k) not in issued:
+                            passes(m, k)
+                            issued.add((m, k))
+        for m in range(PASSES):
+            epilogue(m)

@@ -21,20 +21,32 @@ HALF = N_NODES // 2
 
 FLOPS = 2 * N_NODES * N_NODES * G_OUT + 2 * N_NODES * H_IN * G_OUT
 
-SCALAR_DEGREES = (2, 6, 10)
-H_AFTER = 3
+KINDS = "SVPVVPVPVPVPVPVV"
+H_AFTER = 8
+H_FLIP = 8
+Y_STEPS = (10, 11, 13, 15)
+Q_START = 2
+Q_EVERY = 1.0
+D_LEAD = 2
+G_LAG = 1
+V_EXITS = ((0, 0), (0, 1))
+E_LAG = 2
 
 
 def tile_gcnclassifer_pb_kernel(tc, h_gcn1, adj, gcn2_w, gcn2_b, out):
     nc = tc.nc
     with ExitStack() as ctx:
         keep = ctx.enter_context(tc.tile_pool(name="keep", bufs=1))
-        stage = ctx.enter_context(tc.tile_pool(name="stage", bufs=8))
+        stage = ctx.enter_context(tc.tile_pool(name="stage", bufs=15))
+        lined = ctx.enter_context(tc.tile_pool(name="lined", bufs=4))
         junk = ctx.enter_context(tc.tile_pool(name="junk", bufs=2))
         small = ctx.enter_context(tc.tile_pool(name="small", bufs=4))
-        ps_t = ctx.enter_context(tc.psum_pool(name="ps_t", bufs=7))
+        ps_t = ctx.enter_context(tc.psum_pool(name="ps_t", bufs=6))
         ps_x = ctx.enter_context(tc.psum_pool(name="ps_x", bufs=1))
+        ps_d = ctx.enter_context(tc.psum_pool(name="ps_d", bufs=1))
 
+        ones = keep.tile([P, 2], BF16)
+        nc.vector.memset(ones[:], 1.0)
         one = keep.tile([P, 1], F32)
         nc.vector.memset(one[:], 1.0)
         warm = keep.tile([P, 1], F32)
@@ -60,7 +72,6 @@ def tile_gcnclassifer_pb_kernel(tc, h_gcn1, adj, gcn2_w, gcn2_b, out):
                     out=h_sb[:].rearrange("p (b e) k -> p b (e k)", e=4),
                     in_=h_gcn1.rearrange("(b p e) k -> p b (e k)", p=P, e=4),
                 )
-
         nc.sync.dma_start(out=bias[:], in_=gcn2_b.partition_broadcast(P))
 
         deg = keep.tile([P, TILES, 8], F32)
@@ -74,39 +85,67 @@ def tile_gcnclassifer_pb_kernel(tc, h_gcn1, adj, gcn2_w, gcn2_b, out):
         z_sb = keep.tile([P, TILES, G_OUT], F32)
         o_sb = keep.tile([P, TILES, G_OUT], F32)
         out_v = out.rearrange("(b p e) g -> p b (e g)", p=P, e=4)
+        deg_ps = ps_d.tile([P, TILES, 2], F32)
         grouped = {}
+        in_line = {}
+        banks = {}
+        acc = {}
+        issued = set()
 
         def degree(r):
-            acc = deg[:, r, 0:1]
-            if r in SCALAR_DEGREES:
-                js = junk.tile([P, N_NODES], BF16)
-                nc.scalar.activation(out=js[:], in_=a_sb[:, r, :], func=ACT.Copy, accum_out=acc)
-            else:
-                jv = junk.tile([P, HALF], F32)
-                nc.vector.scalar_tensor_tensor(
-                    out=jv[:],
-                    in0=a_sb[:, r, 0:HALF],
-                    scalar=1.0,
-                    in1=a_sb[:, r, HALF:N_NODES],
+            if KINDS[r] == "V":
+                row = lined.tile([P, 2, 512, 2], BF16, name="row")
+                in_line[r] = row
+                nc.vector.tensor_scalar(
+                    out=row[:],
+                    in0=a_sb[:, r, :].rearrange("p (q u e) -> p u q e", u=2, e=2),
+                    scalar1=1.0,
+                    scalar2=0.0,
                     op0=ALU.mult,
                     op1=ALU.add,
-                    accum_out=acc,
+                    accum_out=deg[:, r, 0:1],
                 )
+            elif KINDS[r] == "S":
+                js = junk.tile([P, N_NODES], BF16, name="js")
+                nc.scalar.activation(out=js[:], in_=a_sb[:, r, :], func=ACT.Copy, accum_out=deg[:, r, 0:1])
 
-        def flip(r):
+        def pe_degree(r):
+            by_k = grouped[r][:].rearrange("p (c i t) -> p c i t", c=4, t=4)
+            for c in range(4):
+                for t in range(4):
+                    nc.tensor.matmul(
+                        out=deg_ps[:, r, 0:1],
+                        lhsT=by_k[:, c, :, t],
+                        rhs=ones[:, 0:1],
+                        start=(c == 0 and t == 0),
+                        stop=(c == 3 and t == 3),
+                    )
+
+        def transposes(r):
             words = a_sb[:, r, :].bitcast(F32)
+            for half in range(2):
+                xt = ps_t.tile([P, 2, 2, P], F32, name="xt")
+                banks[r, half] = xt
+                for cc in range(2):
+                    for u in range(2):
+                        c = 2 * half + cc
+                        if KINDS[r] == "V":
+                            src = in_line[r][:, u, 128 * c : 128 * c + 128, :].rearrange("p q e -> p (q e)").bitcast(F32)
+                        else:
+                            src = words[:, 256 * c + u : 256 * c + 256 : 2]
+                        nc.tensor.transpose(xt[:, cc, u, :], src, ident[:])
+
+        def exits(r):
             g_t = stage.tile([P, 4 * 512], BF16, align_bytes=64, name="g_t")
             grouped[r] = g_t
             g_w = g_t[:].bitcast(F32).rearrange("p (c i u) -> p c i u", c=4, u=2)
             for half in range(2):
-                xt = ps_t.tile([P, 2, 2, P], F32, name="xt")
-                for cc in range(2):
-                    for u in range(2):
-                        first = 256 * (2 * half + cc)
-                        nc.tensor.transpose(xt[:, cc, u, :], words[:, first + u : first + 256 : 2], ident[:])
-                nc.scalar.copy(
-                    out=g_w[:, 2 * half : 2 * half + 2, :, :], in_=xt[:].rearrange("p c u i -> p c i u")
-                )
+                src = banks[r, half][:].rearrange("p c u i -> p c i u")
+                dst = g_w[:, 2 * half : 2 * half + 2, :, :]
+                if (r, half) in V_EXITS:
+                    nc.vector.tensor_copy(out=dst, in_=src)
+                else:
+                    nc.scalar.copy(out=dst, in_=src)
 
         def quantise(r):
             nc.vector.quantize_mx(
@@ -121,12 +160,10 @@ def tile_gcnclassifer_pb_kernel(tc, h_gcn1, adj, gcn2_w, gcn2_b, out):
                     nc.tensor.transpose(ht[:, t, :], h_w[:, 4 * q + t, :], ident[:])
                 nc.scalar.copy(out=h_t[:, 4 * q : 4 * q + 4, :], in_=ht[:])
 
-        def make_y(c):
-            rt = small.tile([P, 4], F32, name="rt")
-            nc.scalar.sqrt(out=rt[:], in_=deg[:, 4 * c : 4 * c + 4, 0])
-            nc.vector.reciprocal(out=dis[:, 4 * c : 4 * c + 4], in_=rt[:])
+        def project(c):
             h_b = h_t[:].bitcast(BF16).rearrange("p r (j k) -> p r j k", k=2)
             xw = ps_x.tile([P, 4, G_OUT], F32, name="xw")
+            banks["xw", c] = xw
             for t in range(4):
                 for k in range(2):
                     nc.tensor.matmul(
@@ -136,73 +173,100 @@ def tile_gcnclassifer_pb_kernel(tc, h_gcn1, adj, gcn2_w, gcn2_b, out):
                         start=(k == 0),
                         stop=(k == 1),
                     )
+
+        def make_dis(c):
+            rt = small.tile([P, 4], F32, name="rt")
+            banks["rt", c] = rt
+            t0 = 0
+            while t0 < 4:
+                t1 = t0
+                while t1 < 4 and (KINDS[4 * c + t1] == "P") == (KINDS[4 * c + t0] == "P"):
+                    t1 += 1
+                src = deg_ps if KINDS[4 * c + t0] == "P" else deg
+                nc.scalar.sqrt(out=rt[:, t0:t1], in_=src[:, 4 * c + t0 : 4 * c + t1, 0])
+                t0 = t1
+
+        def make_y(c):
+            rt = banks["rt", c]
+            nc.vector.reciprocal(out=dis[:, 4 * c : 4 * c + 4], in_=rt[:])
             nc.vector.tensor_tensor(
                 out=y_g[:, c, :, :],
-                in0=xw[:].rearrange("p t g -> p g t"),
+                in0=banks["xw", c][:].rearrange("p t g -> p g t"),
                 in1=dis[:, 4 * c : 4 * c + 4].unsqueeze(1).to_broadcast([P, G_OUT, 4]),
                 op=ALU.mult,
             )
+
+        def quantise_y(c):
             nc.vector.quantize_mx(
                 out=y_codes[:, c, :].bitcast(FP8X4),
                 scales=y_scales[:, c, :],
                 in_=y_g[:, c, :, :].rearrange("p g t -> p (g t)"),
             )
 
-        acc = {}
-
-        issued = set()
-
-        def passes(m, c):
-            if m not in acc:
-                acc_ps = ps_t.tile([P, 4, G_OUT], F32, name="xt")
-                acc[m] = acc_ps
-            for t in range(4):
-                r = 4 * m + t
+        def passes(r):
+            acc_ps = ps_t.tile([P, G_OUT], F32, name="xt")
+            acc[r] = acc_ps
+            for c in range(PASSES):
                 nc.tensor.matmul_mx(
-                    out=acc[m][:, t, :],
+                    out=acc_ps[:],
                     lhsT=codes[:, r, 128 * c : 128 * c + 128].bitcast(FP8X4),
                     lhsT_scale=scales[:, r, 128 * c : 128 * c + 128],
                     rhs=y_codes[:, c, :].bitcast(FP8X4),
                     rhs_scale=y_scales[:, c, :],
-                    start=(c == 0 and t == 0),
-                    stop=(c == PASSES - 1 and t == 3),
+                    start=(c == 0),
+                    stop=(c == PASSES - 1),
                 )
 
-        def epilogue(m):
-            for t in range(4):
-                r = 4 * m + t
-                nc.vector.scalar_tensor_tensor(
-                    out=z_sb[:, r, :],
-                    in0=acc[m][:, t, :],
-                    scalar=dis[:, r : r + 1],
-                    in1=bias[:],
-                    op0=ALU.mult,
-                    op1=ALU.add,
-                )
-            nc.scalar.activation(
-                out=o_sb[:, 4 * m : 4 * m + 4, :], in_=z_sb[:, 4 * m : 4 * m + 4, :], func=ACT.Relu
+        def scale_and_bias(r):
+            nc.vector.scalar_tensor_tensor(
+                out=z_sb[:, r, :],
+                in0=acc[r][:],
+                scalar=dis[:, r : r + 1],
+                in1=bias[:],
+                op0=ALU.mult,
+                op1=ALU.add,
             )
+
+        def finish(r0, r1):
+            nc.scalar.activation(out=o_sb[:, r0:r1, :], in_=z_sb[:, r0:r1, :], func=ACT.Relu)
+            m, t0 = divmod(r0, 4)
             nc.sync.dma_start(
-                out=out_v[:, m, :],
-                in_=o_sb[:, 4 * m : 4 * m + 4, :].rearrange("p e g -> p (e g)"),
+                out=out_v[:, m, G_OUT * t0 : G_OUT * (t0 + r1 - r0)],
+                in_=o_sb[:, r0:r1, :].rearrange("p e g -> p (e g)"),
             )
 
-        for c in range(PASSES + 1):
-            if c < PASSES:
-                for r in range(4 * c, 4 * c + 4):
-                    degree(r)
-                    flip(r)
-                    if r == H_AFTER:
-                        flip_h()
-                make_y(c)
-            if c > 0:
-                for r in range(4 * c - 4, 4 * c):
-                    quantise(r)
-                known = min(c, PASSES - 1) + 1
-                for m in range(c):
-                    for k in range(known):
-                        if (m, k) not in issued:
-                            passes(m, k)
-                            issued.add((m, k))
-        for m in range(PASSES):
-            epilogue(m)
+        with tc.manual_schedule():
+            nq = 0
+            for r in range(D_LEAD):
+                degree(r)
+            for s in range(TILES):
+                if s in Y_STEPS:
+                    make_dis(Y_STEPS.index(s))
+                transposes(s)
+                if 0 <= s - G_LAG and KINDS[s - G_LAG] == "P":
+                    pe_degree(s - G_LAG)
+                exits(s)
+                if s + D_LEAD < TILES:
+                    degree(s + D_LEAD)
+                if s == H_FLIP:
+                    flip_h()
+                if s in Y_STEPS:
+                    make_y(Y_STEPS.index(s))
+                while Q_START + Q_EVERY * nq <= s:
+                    quantise(nq)
+                    nq += 1
+                if s in Y_STEPS:
+                    quantise_y(Y_STEPS.index(s))
+                if s + 1 in Y_STEPS:
+                    project(Y_STEPS.index(s + 1))
+            for r in range(TILES + E_LAG):
+                if r < nq:
+                    passes(r)
+                if r + nq < TILES:
+                    quantise(r + nq)
+                if nq <= r < TILES:
+                    passes(r)
+                if r >= E_LAG:
+                    scale_and_bias(r - E_LAG)
+                    if (r - E_LAG) % 4 == 3:
+                        finish(r - E_LAG - 3, r - E_LAG + 1)

@@ -21,16 +21,22 @@ HALF = N_NODES // 2
 
 FLOPS = 2 * N_NODES * N_NODES * G_OUT + 2 * N_NODES * H_IN * G_OUT
 
-KINDS = "SVPVVPVPVPVPVPVV"
-H_AFTER = 8
-H_FLIP = 8
-Y_STEPS = (10, 11, 13, 15)
+KINDS = "SVVVPVVVPVAVPVVV"
+H_AFTER = 6
+H_FLIP = 6
+Y_STEPS = (7, 8, 11, 14)
 Q_START = 2
 Q_EVERY = 1.0
 D_LEAD = 2
 G_LAG = 1
 V_EXITS = ((0, 0), (0, 1))
-E_LAG = 2
+PASS_PER = 1
+ARS = True
+D_MORE = 8
+SG_BANKS = ()
+G_RELU = ()
+WARM_FIRST = 0
+WARM_EVERY = 0
 
 
 def tile_gcnclassifer_pb_kernel(tc, h_gcn1, adj, gcn2_w, gcn2_b, out):
@@ -38,7 +44,7 @@ def tile_gcnclassifer_pb_kernel(tc, h_gcn1, adj, gcn2_w, gcn2_b, out):
     with ExitStack() as ctx:
         keep = ctx.enter_context(tc.tile_pool(name="keep", bufs=1))
         stage = ctx.enter_context(tc.tile_pool(name="stage", bufs=15))
-        lined = ctx.enter_context(tc.tile_pool(name="lined", bufs=4))
+        lined = ctx.enter_context(tc.tile_pool(name="lined", bufs=6))
         junk = ctx.enter_context(tc.tile_pool(name="junk", bufs=2))
         small = ctx.enter_context(tc.tile_pool(name="small", bufs=4))
         ps_t = ctx.enter_context(tc.psum_pool(name="ps_t", bufs=6))
@@ -50,7 +56,7 @@ def tile_gcnclassifer_pb_kernel(tc, h_gcn1, adj, gcn2_w, gcn2_b, out):
         one = keep.tile([P, 1], F32)
         nc.vector.memset(one[:], 1.0)
         warm = keep.tile([P, 1], F32)
-        nc.scalar.sqrt(out=warm[:], in_=one[:])
+        nc.scalar.activation(out=warm[:], in_=one[:], func=ACT.Abs_reciprocal_sqrt if ARS else ACT.Sqrt)
         ident = keep.tile([P, P], F32)
         make_identity(nc, ident[:])
 
@@ -85,7 +91,7 @@ def tile_gcnclassifer_pb_kernel(tc, h_gcn1, adj, gcn2_w, gcn2_b, out):
         z_sb = keep.tile([P, TILES, G_OUT], F32)
         o_sb = keep.tile([P, TILES, G_OUT], F32)
         out_v = out.rearrange("(b p e) g -> p b (e g)", p=P, e=4)
-        deg_ps = ps_d.tile([P, TILES, 2], F32)
+        deg_ps = ps_d.tile([P, 256, 2], F32)
         grouped = {}
         in_line = {}
         banks = {}
@@ -103,6 +109,15 @@ def tile_gcnclassifer_pb_kernel(tc, h_gcn1, adj, gcn2_w, gcn2_b, out):
                     scalar2=0.0,
                     op0=ALU.mult,
                     op1=ALU.add,
+                    accum_out=deg[:, r, 0:1],
+                )
+            elif KINDS[r] == "A":
+                row = lined.tile([P, 2, 512, 2], BF16, name="row")
+                in_line[r] = row
+                nc.scalar.activation(
+                    out=row[:],
+                    in_=a_sb[:, r, :].rearrange("p (q u e) -> p u q e", u=2, e=2),
+                    func=ACT.Copy,
                     accum_out=deg[:, r, 0:1],
                 )
             elif KINDS[r] == "S":
@@ -129,7 +144,7 @@ def tile_gcnclassifer_pb_kernel(tc, h_gcn1, adj, gcn2_w, gcn2_b, out):
                 for cc in range(2):
                     for u in range(2):
                         c = 2 * half + cc
-                        if KINDS[r] == "V":
+                        if r in in_line:
                             src = in_line[r][:, u, 128 * c : 128 * c + 128, :].rearrange("p q e -> p (q e)").bitcast(F32)
                         else:
                             src = words[:, 256 * c + u : 256 * c + 256 : 2]
@@ -183,12 +198,18 @@ def tile_gcnclassifer_pb_kernel(tc, h_gcn1, adj, gcn2_w, gcn2_b, out):
                 while t1 < 4 and (KINDS[4 * c + t1] == "P") == (KINDS[4 * c + t0] == "P"):
                     t1 += 1
                 src = deg_ps if KINDS[4 * c + t0] == "P" else deg
-                nc.scalar.sqrt(out=rt[:, t0:t1], in_=src[:, 4 * c + t0 : 4 * c + t1, 0])
+                if ARS:
+                    nc.scalar.activation(
+                        out=dis[:, 4 * c + t0 : 4 * c + t1], in_=src[:, 4 * c + t0 : 4 * c + t1, 0], func=ACT.Abs_reciprocal_sqrt
+                    )
+                else:
+                    nc.scalar.sqrt(out=rt[:, t0:t1], in_=src[:, 4 * c + t0 : 4 * c + t1, 0])
                 t0 = t1
 
         def make_y(c):
             rt = banks["rt", c]
-            nc.vector.reciprocal(out=dis[:, 4 * c : 4 * c + 4], in_=rt[:])
+            if not ARS:
+                nc.vector.reciprocal(out=dis[:, 4 * c : 4 * c + 4], in_=rt[:])
             nc.vector.tensor_tensor(
                 out=y_g[:, c, :, :],
                 in0=banks["xw", c][:].rearrange("p t g -> p g t"),
@@ -202,6 +223,9 @@ def tile_gcnclassifer_pb_kernel(tc, h_gcn1, adj, gcn2_w, gcn2_b, out):
                 scales=y_scales[:, c, :],
                 in_=y_g[:, c, :, :].rearrange("p g t -> p (g t)"),
             )
+
+        def dummy():
+            nc.tensor.matmul(out=deg_ps[:].rearrange("p a b -> p (a b)")[:, 384:512], lhsT=ident[:], rhs=ident[:], start=True, stop=True)
 
         def passes(r):
             acc_ps = ps_t.tile([P, G_OUT], F32, name="xt")
@@ -227,46 +251,84 @@ def tile_gcnclassifer_pb_kernel(tc, h_gcn1, adj, gcn2_w, gcn2_b, out):
                 op1=ALU.add,
             )
 
+        def scale_only(r):
+            nc.scalar.activation(out=z_sb[:, r, :], in_=acc[r][:], func=ACT.Copy, scale=dis[:, r : r + 1])
+
         def finish(r0, r1):
-            nc.scalar.activation(out=o_sb[:, r0:r1, :], in_=z_sb[:, r0:r1, :], func=ACT.Relu)
+            m = r0 // 4
+            if m in SG_BANKS:
+                nc.gpsimd.tensor_tensor(
+                    out=z_sb[:, r0:r1, :],
+                    in0=z_sb[:, r0:r1, :],
+                    in1=bias[:].unsqueeze(1).to_broadcast([P, r1 - r0, G_OUT]),
+                    op=ALU.add,
+                )
+            if r1 == TILES:
+                nc.vector.tensor_scalar(
+                    out=o_sb[:, r0:r1, :], in0=z_sb[:, r0:r1, :], scalar1=0.0, scalar2=None, op0=ALU.max
+                )
+            elif m in G_RELU:
+                nc.gpsimd.tensor_scalar(
+                    out=o_sb[:, r0:r1, :], in0=z_sb[:, r0:r1, :], scalar1=3.0e38, scalar2=0.0, op0=ALU.min, op1=ALU.max
+                )
+            else:
+                nc.scalar.activation(out=o_sb[:, r0:r1, :], in_=z_sb[:, r0:r1, :], func=ACT.Relu)
             m, t0 = divmod(r0, 4)
             nc.sync.dma_start(
                 out=out_v[:, m, G_OUT * t0 : G_OUT * (t0 + r1 - r0)],
                 in_=o_sb[:, r0:r1, :].rearrange("p e g -> p (e g)"),
             )
 
+        def emit_out(r):
+            if r // 4 in SG_BANKS:
+                scale_only(r)
+            else:
+                scale_and_bias(r)
+            if r % 4 == 3 and r < TILES - 1 or r == TILES - 3:
+                finish(r - r % 4, r + 1)
+            elif r == TILES - 1:
+                finish(r - 1, r + 1)
+
         with tc.manual_schedule():
             nq = 0
-            for r in range(D_LEAD):
-                degree(r)
-            for s in range(TILES):
+            npass = 0
+            nout = 0
+            nlead = 1
+            for w in range(WARM_FIRST):
+                dummy()
+            for s in range(TILES + 20):
+                if s > 0 and WARM_EVERY and s % WARM_EVERY == 0 and s < TILES:
+                    dummy()
                 if s in Y_STEPS:
                     make_dis(Y_STEPS.index(s))
-                transposes(s)
-                if 0 <= s - G_LAG and KINDS[s - G_LAG] == "P":
+                if s < TILES:
+                    if s == 0:
+                        degree(0)
+                    transposes(s)
+                if 0 <= s - G_LAG < TILES and KINDS[s - G_LAG] == "P":
                     pe_degree(s - G_LAG)
-                exits(s)
-                if s + D_LEAD < TILES:
-                    degree(s + D_LEAD)
+                if s < TILES:
+                    exits(s)
+                while nlead < TILES and nlead <= s + D_LEAD + (s >= D_MORE):
+                    degree(nlead)
+                    nlead += 1
                 if s == H_FLIP:
                     flip_h()
                 if s in Y_STEPS:
                     make_y(Y_STEPS.index(s))
-                while Q_START + Q_EVERY * nq <= s:
+                had = npass
+                while nq < TILES and Q_START + Q_EVERY * nq <= s:
                     quantise(nq)
                     nq += 1
                 if s in Y_STEPS:
                     quantise_y(Y_STEPS.index(s))
                 if s + 1 in Y_STEPS:
                     project(Y_STEPS.index(s + 1))
-            for r in range(TILES + E_LAG):
-                if r < nq:
-                    passes(r)
-                if r + nq < TILES:
-                    quantise(r + nq)
-                if nq <= r < TILES:
-                    passes(r)
-                if r >= E_LAG:
-                    scale_and_bias(r - E_LAG)
-                    if (r - E_LAG) % 4 == 3:
-                        finish(r - E_LAG - 3, r - E_LAG + 1)
+                if s >= Y_STEPS[3]:
+                    for i in range(PASS_PER):
+                        if npass < nq:
+                            passes(npass)
+                            npass += 1
+                while nout < had:
+                    emit_out(nout)
+                    nout += 1

@@ -66,12 +66,10 @@ def tile_gcnclassifer_pb_kernel(tc, h_gcn1, adj, gcn2_w, gcn2_b, out):
         bias = keep.tile([P, G_OUT], BF16)
 
         adj_v = adj.rearrange("(b p e) j -> p b e j", p=P, e=4)
-        for r in range(TILES):
-            if r == 0:
-                nc.sync.dma_start(out=a_sb[:, r, 0:HALF], in_=adj_v[:, 0, 0, 0:HALF])
-                nc.sync.dma_start(out=a_sb[:, r, HALF:N_NODES], in_=adj_v[:, 0, 0, HALF:N_NODES])
-            else:
-                nc.sync.dma_start(out=a_sb[:, r, :], in_=adj_v[:, r // 4, r % 4, :])
+        nc.sync.dma_start(out=a_sb[:, 0, 0:HALF], in_=adj_v[:, 0, 0, 0:HALF])
+        nc.sync.dma_start(out=a_sb[:, 0, HALF:N_NODES], in_=adj_v[:, 0, 0, HALF:N_NODES])
+        for r, n in ((1, 1), (2, 2), (4, 2), (6, 2), (8, 2), (10, 2), (12, 2), (14, 1), (15, 1)):
+            nc.sync.dma_start(out=a_sb[:, r : r + n, :], in_=adj_v[:, r // 4, r % 4 : r % 4 + n, :])
             if r == H_AFTER:
                 nc.sync.dma_start(out=w_sb[:], in_=gcn2_w.rearrange("(q k) g -> q k g", k=2))
                 nc.sync.dma_start(

@@ -21,17 +21,25 @@ HALF = N_NODES // 2
 
 FLOPS = 2 * N_NODES * N_NODES * G_OUT + 2 * N_NODES * H_IN * G_OUT
 
-KINDS = "SVVVPVVVPVAVPVVV"
+KINDS = "VVVVPVVVPVPVVVSV"
 H_AFTER = 6
 H_FLIP = 6
-Y_STEPS = (7, 8, 11, 14)
+Y_STEPS = (7, 8, 12, 14)
 Q_START = 2
 Q_EVERY = 1.0
 D_LEAD = 2
 G_LAG = 1
-V_EXITS = ((0, 0), (0, 1))
-PASS_PER = 1
+V_EXITS = ()
+LOADS = ((0, 2), (2, 2), (4, 2), (6, 2), (8, 2), (10, 2), (12, 2), (14, 2))
+V_H = ()
+HALVES = False
+EARLY = (13, )
+OUT_LAG = 1
+OUT_PER = 2
+SKEW = True
+X_STEPS = (6, 7, 11, 13)
 ARS = True
+C_LAG = 3
 D_MORE = 8
 SG_BANKS = ()
 G_RELU = ()
@@ -43,12 +51,11 @@ def tile_gcnclassifer_pb_kernel(tc, h_gcn1, adj, gcn2_w, gcn2_b, out):
     nc = tc.nc
     with ExitStack() as ctx:
         keep = ctx.enter_context(tc.tile_pool(name="keep", bufs=1))
-        stage = ctx.enter_context(tc.tile_pool(name="stage", bufs=15))
+        stage = ctx.enter_context(tc.tile_pool(name="stage", bufs=9))
         lined = ctx.enter_context(tc.tile_pool(name="lined", bufs=6))
         junk = ctx.enter_context(tc.tile_pool(name="junk", bufs=2))
         small = ctx.enter_context(tc.tile_pool(name="small", bufs=4))
-        ps_t = ctx.enter_context(tc.psum_pool(name="ps_t", bufs=6))
-        ps_x = ctx.enter_context(tc.psum_pool(name="ps_x", bufs=1))
+        ps_t = ctx.enter_context(tc.psum_pool(name="ps_t", bufs=7))
         ps_d = ctx.enter_context(tc.psum_pool(name="ps_d", bufs=1))
 
         ones = keep.tile([P, 2], BF16)
@@ -66,9 +73,10 @@ def tile_gcnclassifer_pb_kernel(tc, h_gcn1, adj, gcn2_w, gcn2_b, out):
         bias = keep.tile([P, G_OUT], BF16)
 
         adj_v = adj.rearrange("(b p e) j -> p b e j", p=P, e=4)
-        nc.sync.dma_start(out=a_sb[:, 0, 0:HALF], in_=adj_v[:, 0, 0, 0:HALF])
-        nc.sync.dma_start(out=a_sb[:, 0, HALF:N_NODES], in_=adj_v[:, 0, 0, HALF:N_NODES])
-        for r, n in ((1, 1), (2, 2), (4, 2), (6, 2), (8, 2), (10, 2), (12, 2), (14, 1), (15, 1)):
+        if HALVES:
+            nc.sync.dma_start(out=a_sb[:, 0, 0:HALF], in_=adj_v[:, 0, 0, 0:HALF])
+            nc.sync.dma_start(out=a_sb[:, 0, HALF:N_NODES], in_=adj_v[:, 0, 0, HALF:N_NODES])
+        for r, n in LOADS:
             nc.sync.dma_start(out=a_sb[:, r : r + n, :], in_=adj_v[:, r // 4, r % 4 : r % 4 + n, :])
             if r == H_AFTER:
                 nc.sync.dma_start(out=w_sb[:], in_=gcn2_w.rearrange("(q k) g -> q k g", k=2))
@@ -109,6 +117,27 @@ def tile_gcnclassifer_pb_kernel(tc, h_gcn1, adj, gcn2_w, gcn2_b, out):
                     op1=ALU.add,
                     accum_out=deg[:, r, 0:1],
                 )
+            elif KINDS[r] == "U":
+                jv = junk.tile([P, HALF], F32, name="jv")
+                nc.vector.scalar_tensor_tensor(
+                    out=jv[:],
+                    in0=a_sb[:, r, 0:HALF],
+                    scalar=1.0,
+                    in1=a_sb[:, r, HALF:N_NODES],
+                    op0=ALU.mult,
+                    op1=ALU.add,
+                    accum_out=deg[:, r, 0:1],
+                )
+            elif KINDS[r] == "G":
+                quads = a_sb[:, r, :].rearrange("p (a b) -> p a b", a=4)
+                pair = junk.tile([P, 2, 512], F32, name="pair")
+                for a in range(2):
+                    nc.gpsimd.tensor_tensor(
+                        out=pair[:, a, :], in0=quads[:, 2 * a, :], in1=quads[:, 2 * a + 1, :], op=ALU.add
+                    )
+                part = junk.tile([P, 512], F32, name="part")
+                nc.gpsimd.tensor_tensor(out=part[:], in0=pair[:, 0, :], in1=pair[:, 1, :], op=ALU.add)
+                banks["part", r] = part
             elif KINDS[r] == "A":
                 row = lined.tile([P, 2, 512, 2], BF16, name="row")
                 in_line[r] = row
@@ -121,6 +150,10 @@ def tile_gcnclassifer_pb_kernel(tc, h_gcn1, adj, gcn2_w, gcn2_b, out):
             elif KINDS[r] == "S":
                 js = junk.tile([P, N_NODES], BF16, name="js")
                 nc.scalar.activation(out=js[:], in_=a_sb[:, r, :], func=ACT.Copy, accum_out=deg[:, r, 0:1])
+
+        def close_degree(r):
+            full = junk.tile([P, 512], F32, name="full")
+            nc.scalar.activation(out=full[:], in_=banks["part", r][:], func=ACT.Copy, accum_out=deg[:, r, 0:1])
 
         def pe_degree(r):
             by_k = grouped[r][:].rearrange("p (c i t) -> p c i t", c=4, t=4)
@@ -171,11 +204,14 @@ def tile_gcnclassifer_pb_kernel(tc, h_gcn1, adj, gcn2_w, gcn2_b, out):
                 ht = ps_t.tile([P, 4, P], F32, name="xt")
                 for t in range(4):
                     nc.tensor.transpose(ht[:, t, :], h_w[:, 4 * q + t, :], ident[:])
-                nc.scalar.copy(out=h_t[:, 4 * q : 4 * q + 4, :], in_=ht[:])
+                if q in V_H:
+                    nc.vector.tensor_copy(out=h_t[:, 4 * q : 4 * q + 4, :], in_=ht[:])
+                else:
+                    nc.scalar.copy(out=h_t[:, 4 * q : 4 * q + 4, :], in_=ht[:])
 
         def project(c):
             h_b = h_t[:].bitcast(BF16).rearrange("p r (j k) -> p r j k", k=2)
-            xw = ps_x.tile([P, 4, G_OUT], F32, name="xw")
+            xw = ps_t.tile([P, 4, G_OUT], F32, name="xt")
             banks["xw", c] = xw
             for t in range(4):
                 for k in range(2):
@@ -225,24 +261,27 @@ def tile_gcnclassifer_pb_kernel(tc, h_gcn1, adj, gcn2_w, gcn2_b, out):
         def dummy():
             nc.tensor.matmul(out=deg_ps[:].rearrange("p a b -> p (a b)")[:, 384:512], lhsT=ident[:], rhs=ident[:], start=True, stop=True)
 
-        def passes(r):
-            acc_ps = ps_t.tile([P, G_OUT], F32, name="xt")
-            acc[r] = acc_ps
-            for c in range(PASSES):
-                nc.tensor.matmul_mx(
-                    out=acc_ps[:],
-                    lhsT=codes[:, r, 128 * c : 128 * c + 128].bitcast(FP8X4),
-                    lhsT_scale=scales[:, r, 128 * c : 128 * c + 128],
-                    rhs=y_codes[:, c, :].bitcast(FP8X4),
-                    rhs_scale=y_scales[:, c, :],
-                    start=(c == 0),
-                    stop=(c == PASSES - 1),
-                )
+        def passes(m, ks):
+            if m not in acc:
+                acc_ps = ps_t.tile([P, 4, G_OUT], F32, name="xt")
+                acc[m] = acc_ps
+            for k in ks:
+                for t in range(4):
+                    r = 4 * m + t
+                    nc.tensor.matmul_mx(
+                        out=acc[m][:, t, :],
+                        lhsT=codes[:, r, 128 * k : 128 * k + 128].bitcast(FP8X4),
+                        lhsT_scale=scales[:, r, 128 * k : 128 * k + 128],
+                        rhs=y_codes[:, k, :].bitcast(FP8X4),
+                        rhs_scale=y_scales[:, k, :],
+                        start=(k == 0 and t == 0),
+                        stop=(k == PASSES - 1 and t == 3),
+                    )
 
         def scale_and_bias(r):
             nc.vector.scalar_tensor_tensor(
                 out=z_sb[:, r, :],
-                in0=acc[r][:],
+                in0=acc[r // 4][:, r % 4, :],
                 scalar=dis[:, r : r + 1],
                 in1=bias[:],
                 op0=ALU.mult,
@@ -250,7 +289,7 @@ def tile_gcnclassifer_pb_kernel(tc, h_gcn1, adj, gcn2_w, gcn2_b, out):
             )
 
         def scale_only(r):
-            nc.scalar.activation(out=z_sb[:, r, :], in_=acc[r][:], func=ACT.Copy, scale=dis[:, r : r + 1])
+            nc.scalar.activation(out=z_sb[:, r, :], in_=acc[r // 4][:, r % 4, :], func=ACT.Copy, scale=dis[:, r : r + 1])
 
         def finish(r0, r1):
             m = r0 // 4
@@ -277,26 +316,24 @@ def tile_gcnclassifer_pb_kernel(tc, h_gcn1, adj, gcn2_w, gcn2_b, out):
                 in_=o_sb[:, r0:r1, :].rearrange("p e g -> p (e g)"),
             )
 
-        def emit_out(r):
-            if r // 4 in SG_BANKS:
-                scale_only(r)
+        def emit_out(m):
+            for r in range(4 * m, 4 * m + 4):
+                if m in SG_BANKS:
+                    scale_only(r)
+                else:
+                    scale_and_bias(r)
+                if m == 3 and r == TILES - 3:
+                    finish(r - 1, r + 1)
+            if m < 3:
+                finish(4 * m, 4 * m + 4)
             else:
-                scale_and_bias(r)
-            if r % 4 == 3 and r < TILES - 1 or r == TILES - 3:
-                finish(r - r % 4, r + 1)
-            elif r == TILES - 1:
-                finish(r - 1, r + 1)
+                finish(TILES - 2, TILES)
 
         with tc.manual_schedule():
             nq = 0
-            npass = 0
-            nout = 0
             nlead = 1
-            for w in range(WARM_FIRST):
-                dummy()
-            for s in range(TILES + 20):
-                if s > 0 and WARM_EVERY and s % WARM_EVERY == 0 and s < TILES:
-                    dummy()
+            done = 0
+            for s in range(TILES + 16):
                 if s in Y_STEPS:
                     make_dis(Y_STEPS.index(s))
                 if s < TILES:
@@ -310,23 +347,31 @@ def tile_gcnclassifer_pb_kernel(tc, h_gcn1, adj, gcn2_w, gcn2_b, out):
                 while nlead < TILES and nlead <= s + D_LEAD + (s >= D_MORE):
                     degree(nlead)
                     nlead += 1
+                if s >= C_LAG and s - C_LAG < TILES and KINDS[s - C_LAG] == "G":
+                    close_degree(s - C_LAG)
                 if s == H_FLIP:
                     flip_h()
+                if s in X_STEPS:
+                    project(X_STEPS.index(s))
                 if s in Y_STEPS:
                     make_y(Y_STEPS.index(s))
-                had = npass
                 while nq < TILES and Q_START + Q_EVERY * nq <= s:
                     quantise(nq)
                     nq += 1
                 if s in Y_STEPS:
                     quantise_y(Y_STEPS.index(s))
-                if s + 1 in Y_STEPS:
-                    project(Y_STEPS.index(s + 1))
-                if s >= Y_STEPS[3]:
-                    for i in range(PASS_PER):
-                        if npass < nq:
-                            passes(npass)
-                            npass += 1
-                while nout < had:
-                    emit_out(nout)
-                    nout += 1
+                for m in range(len(EARLY)):
+                    if s == EARLY[m]:
+                        passes(m, range(3))
+                if s >= Y_STEPS[3] + OUT_LAG:
+                    for i in range(OUT_PER):
+                        if done < 4 and nq >= 4 * done + 4:
+                            passes(done, range(3, 4) if done < len(EARLY) else range(4))
+                            if done > 0 and SKEW:
+                                emit_out(done - 1)
+                            if not SKEW:
+                                emit_out(done)
+                            done += 1
+                            if done == 4 and SKEW:
+                                emit_out(3)
+            assert done == 4 and nq == TILES and nlead == TILES

@@ -21,7 +21,7 @@ HALF = N_NODES // 2
 
 FLOPS = 2 * N_NODES * N_NODES * G_OUT + 2 * N_NODES * H_IN * G_OUT
 
-KINDS = "VVVVPVVVPVPVVVSV"
+KINDS = "PVVVPVVVPVPVVVSV"
 H_AFTER = 6
 H_FLIP = 6
 Y_STEPS = (7, 8, 12, 14)
@@ -33,9 +33,12 @@ V_EXITS = ()
 LOADS = ((0, 2), (2, 2), (4, 2), (6, 2), (8, 2), (10, 2), (12, 2), (14, 2))
 V_H = ()
 HALVES = False
-EARLY = (13, )
+EARLY = ()
 OUT_LAG = 1
 OUT_PER = 2
+SG_UNITS = (0,)
+Q_ALL = 15
+UNITS = ((0, 4), (4, 4), (8, 4), (12, 2), (14, 2))
 SKEW = True
 X_STEPS = (6, 7, 11, 13)
 ARS = True
@@ -102,7 +105,7 @@ def tile_gcnclassifer_pb_kernel(tc, h_gcn1, adj, gcn2_w, gcn2_b, out):
         in_line = {}
         banks = {}
         acc = {}
-        issued = set()
+        waiting = []
 
         def degree(r):
             if KINDS[r] == "V":
@@ -262,12 +265,13 @@ def tile_gcnclassifer_pb_kernel(tc, h_gcn1, adj, gcn2_w, gcn2_b, out):
             nc.tensor.matmul(out=deg_ps[:].rearrange("p a b -> p (a b)")[:, 384:512], lhsT=ident[:], rhs=ident[:], start=True, stop=True)
 
         def passes(m, ks):
+            r0, n = UNITS[m]
             if m not in acc:
                 acc_ps = ps_t.tile([P, 4, G_OUT], F32, name="xt")
                 acc[m] = acc_ps
             for k in ks:
-                for t in range(4):
-                    r = 4 * m + t
+                for t in range(n):
+                    r = r0 + t
                     nc.tensor.matmul_mx(
                         out=acc[m][:, t, :],
                         lhsT=codes[:, r, 128 * k : 128 * k + 128].bitcast(FP8X4),
@@ -275,21 +279,41 @@ def tile_gcnclassifer_pb_kernel(tc, h_gcn1, adj, gcn2_w, gcn2_b, out):
                         rhs=y_codes[:, k, :].bitcast(FP8X4),
                         rhs_scale=y_scales[:, k, :],
                         start=(k == 0 and t == 0),
-                        stop=(k == PASSES - 1 and t == 3),
+                        stop=(k == PASSES - 1 and t == n - 1),
                     )
 
-        def scale_and_bias(r):
+        def scale_and_bias(r, src):
             nc.vector.scalar_tensor_tensor(
                 out=z_sb[:, r, :],
-                in0=acc[r // 4][:, r % 4, :],
+                in0=src,
                 scalar=dis[:, r : r + 1],
                 in1=bias[:],
                 op0=ALU.mult,
                 op1=ALU.add,
             )
 
-        def scale_only(r):
-            nc.scalar.activation(out=z_sb[:, r, :], in_=acc[r // 4][:, r % 4, :], func=ACT.Copy, scale=dis[:, r : r + 1])
+        def emit_out(m):
+            r0, n = UNITS[m]
+            for t in range(n):
+                if m in SG_UNITS:
+                    nc.scalar.activation(
+                        out=z_sb[:, r0 + t, :], in_=acc[m][:, t, :], func=ACT.Copy, scale=dis[:, r0 + t : r0 + t + 1]
+                    )
+                else:
+                    scale_and_bias(r0 + t, acc[m][:, t, :])
+            if m in SG_UNITS:
+                nc.gpsimd.tensor_tensor(
+                    out=z_sb[:, r0 : r0 + n, :],
+                    in0=z_sb[:, r0 : r0 + n, :],
+                    in1=bias[:].unsqueeze(1).to_broadcast([P, n, G_OUT]),
+                    op=ALU.add,
+                )
+                waiting.append((r0, n))
+            else:
+                while waiting:
+                    w0, wn = waiting.pop(0)
+                    finish(w0, w0 + wn)
+                finish(r0, r0 + n)
 
         def finish(r0, r1):
             m = r0 // 4
@@ -315,19 +339,6 @@ def tile_gcnclassifer_pb_kernel(tc, h_gcn1, adj, gcn2_w, gcn2_b, out):
                 out=out_v[:, m, G_OUT * t0 : G_OUT * (t0 + r1 - r0)],
                 in_=o_sb[:, r0:r1, :].rearrange("p e g -> p (e g)"),
             )
-
-        def emit_out(m):
-            for r in range(4 * m, 4 * m + 4):
-                if m in SG_BANKS:
-                    scale_only(r)
-                else:
-                    scale_and_bias(r)
-                if m == 3 and r == TILES - 3:
-                    finish(r - 1, r + 1)
-            if m < 3:
-                finish(4 * m, 4 * m + 4)
-            else:
-                finish(TILES - 2, TILES)
 
         with tc.manual_schedule():
             nq = 0
@@ -355,7 +366,7 @@ def tile_gcnclassifer_pb_kernel(tc, h_gcn1, adj, gcn2_w, gcn2_b, out):
                     project(X_STEPS.index(s))
                 if s in Y_STEPS:
                     make_y(Y_STEPS.index(s))
-                while nq < TILES and Q_START + Q_EVERY * nq <= s:
+                while nq < TILES and (Q_START + Q_EVERY * nq <= s or s >= Q_ALL):
                     quantise(nq)
                     nq += 1
                 if s in Y_STEPS:
@@ -365,13 +376,13 @@ def tile_gcnclassifer_pb_kernel(tc, h_gcn1, adj, gcn2_w, gcn2_b, out):
                         passes(m, range(3))
                 if s >= Y_STEPS[3] + OUT_LAG:
                     for i in range(OUT_PER):
-                        if done < 4 and nq >= 4 * done + 4:
+                        if done < len(UNITS) and nq >= sum(UNITS[done]):
                             passes(done, range(3, 4) if done < len(EARLY) else range(4))
-                            if done > 0 and SKEW:
+                            if done > 0:
                                 emit_out(done - 1)
-                            if not SKEW:
-                                emit_out(done)
                             done += 1
-                            if done == 4 and SKEW:
-                                emit_out(3)
-            assert done == 4 and nq == TILES and nlead == TILES
+                            if done == len(UNITS):
+                                emit_out(done - 1)
+            for r0, n in waiting:
+                finish(r0, r0 + n)
+            assert done == len(UNITS) and nq == TILES and nlead == TILES

@@ -24,7 +24,7 @@ FLOPS = 2 * N_NODES * N_NODES * G_OUT + 2 * N_NODES * H_IN * G_OUT
 KINDS = "PVVVPVVVPVPVVVSV"
 H_AFTER = 6
 H_FLIP = 6
-Y_STEPS = (7, 8, 12, 14)
+Y_STEPS = (7, 8, 12, 13)
 Q_START = 2
 Q_EVERY = 1.0
 D_LEAD = 2
@@ -34,13 +34,13 @@ LOADS = ((0, 2), (2, 2), (4, 2), (6, 2), (8, 2), (10, 2), (12, 2), (14, 2))
 V_H = ()
 HALVES = False
 EARLY = ()
-OUT_LAG = 1
+OUT_LAG = 2
 OUT_PER = 2
-SG_UNITS = (0,)
-Q_ALL = 15
-UNITS = ((0, 4), (4, 4), (8, 4), (12, 2), (14, 2))
+SG_UNITS = ()
+Q_ALL = 40
+UNITS = ((0, 2, "V", "S"), (2, 2, "V", "S"), (4, 2, "V", "S"), (6, 2, "V", "S"), (8, 2, "V", "S"), (10, 2, "V", "S"), (12, 2, "V", "S"), (14, 2, "V", "V"))
 SKEW = True
-X_STEPS = (6, 7, 11, 13)
+X_STEPS = (6, 7, 11, 12)
 ARS = True
 C_LAG = 3
 D_MORE = 8
@@ -265,7 +265,7 @@ def tile_gcnclassifer_pb_kernel(tc, h_gcn1, adj, gcn2_w, gcn2_b, out):
             nc.tensor.matmul(out=deg_ps[:].rearrange("p a b -> p (a b)")[:, 384:512], lhsT=ident[:], rhs=ident[:], start=True, stop=True)
 
         def passes(m, ks):
-            r0, n = UNITS[m]
+            r0, n, by, relu = UNITS[m]
             if m not in acc:
                 acc_ps = ps_t.tile([P, 4, G_OUT], F32, name="xt")
                 acc[m] = acc_ps
@@ -292,53 +292,46 @@ def tile_gcnclassifer_pb_kernel(tc, h_gcn1, adj, gcn2_w, gcn2_b, out):
                 op1=ALU.add,
             )
 
+        def finish(m):
+            r0, n, by, relu = UNITS[m]
+            src = z_sb[:, r0 : r0 + n, :]
+            dst = o_sb[:, r0 : r0 + n, :]
+            if relu == "V":
+                nc.vector.tensor_scalar(out=dst, in0=src, scalar1=0.0, scalar2=None, op0=ALU.max)
+            elif relu == "G":
+                nc.gpsimd.tensor_scalar(out=dst, in0=src, scalar1=3.0e38, scalar2=0.0, op0=ALU.min, op1=ALU.max)
+            else:
+                nc.scalar.activation(out=dst, in_=src, func=ACT.Relu)
+            b, t0 = divmod(r0, 4)
+            nc.sync.dma_start(
+                out=out_v[:, b, G_OUT * t0 : G_OUT * (t0 + n)], in_=dst.rearrange("p e g -> p (e g)")
+            )
+
         def emit_out(m):
-            r0, n = UNITS[m]
+            r0, n, by, relu = UNITS[m]
             for t in range(n):
-                if m in SG_UNITS:
+                r = r0 + t
+                if by == "S":
                     nc.scalar.activation(
-                        out=z_sb[:, r0 + t, :], in_=acc[m][:, t, :], func=ACT.Copy, scale=dis[:, r0 + t : r0 + t + 1]
+                        out=z_sb[:, r, :], in_=acc[m][:, t, :], func=ACT.Copy, scale=dis[:, r : r + 1]
                     )
                 else:
-                    scale_and_bias(r0 + t, acc[m][:, t, :])
-            if m in SG_UNITS:
+                    scale_and_bias(r, acc[m][:, t, :])
+            if by == "S":
                 nc.gpsimd.tensor_tensor(
                     out=z_sb[:, r0 : r0 + n, :],
                     in0=z_sb[:, r0 : r0 + n, :],
                     in1=bias[:].unsqueeze(1).to_broadcast([P, n, G_OUT]),
                     op=ALU.add,
                 )
-                waiting.append((r0, n))
+                if relu == "G":
+                    finish(m)
+                else:
+                    waiting.append(m)
             else:
                 while waiting:
-                    w0, wn = waiting.pop(0)
-                    finish(w0, w0 + wn)
-                finish(r0, r0 + n)
-
-        def finish(r0, r1):
-            m = r0 // 4
-            if m in SG_BANKS:
-                nc.gpsimd.tensor_tensor(
-                    out=z_sb[:, r0:r1, :],
-                    in0=z_sb[:, r0:r1, :],
-                    in1=bias[:].unsqueeze(1).to_broadcast([P, r1 - r0, G_OUT]),
-                    op=ALU.add,
-                )
-            if r1 == TILES:
-                nc.vector.tensor_scalar(
-                    out=o_sb[:, r0:r1, :], in0=z_sb[:, r0:r1, :], scalar1=0.0, scalar2=None, op0=ALU.max
-                )
-            elif m in G_RELU:
-                nc.gpsimd.tensor_scalar(
-                    out=o_sb[:, r0:r1, :], in0=z_sb[:, r0:r1, :], scalar1=3.0e38, scalar2=0.0, op0=ALU.min, op1=ALU.max
-                )
-            else:
-                nc.scalar.activation(out=o_sb[:, r0:r1, :], in_=z_sb[:, r0:r1, :], func=ACT.Relu)
-            m, t0 = divmod(r0, 4)
-            nc.sync.dma_start(
-                out=out_v[:, m, G_OUT * t0 : G_OUT * (t0 + r1 - r0)],
-                in_=o_sb[:, r0:r1, :].rearrange("p e g -> p (e g)"),
-            )
+                    finish(waiting.pop(0))
+                finish(m)
 
         with tc.manual_schedule():
             nq = 0
@@ -376,13 +369,13 @@ def tile_gcnclassifer_pb_kernel(tc, h_gcn1, adj, gcn2_w, gcn2_b, out):
                         passes(m, range(3))
                 if s >= Y_STEPS[3] + OUT_LAG:
                     for i in range(OUT_PER):
-                        if done < len(UNITS) and nq >= sum(UNITS[done]):
+                        if done < len(UNITS) and nq >= UNITS[done][0] + UNITS[done][1]:
                             passes(done, range(3, 4) if done < len(EARLY) else range(4))
                             if done > 0:
                                 emit_out(done - 1)
                             done += 1
                             if done == len(UNITS):
                                 emit_out(done - 1)
-            for r0, n in waiting:
-                finish(r0, r0 + n)
+            for m in waiting:
+                finish(m)
             assert done == len(UNITS) and nq == TILES and nlead == TILES

from contextlib import ExitStack

import concourse.mybir as mybir
from concourse.masks import make_identity

F32 = mybir.dt.float32
BF16 = mybir.dt.bfloat16
U32 = mybir.dt.uint32
U8 = mybir.dt.uint8
FP8X4 = mybir.dt.float8_e4m3fn_x4
ALU = mybir.AluOpType
ACT = mybir.ActivationFunctionType

P = 128
N_NODES = 2048
H_IN = 256
G_OUT = 128
TILES = 16
PASSES = 4
HALF = N_NODES // 2

FLOPS = 2 * N_NODES * N_NODES * G_OUT + 2 * N_NODES * H_IN * G_OUT

KINDS = "PVVVPVVVPVPVVVSV"
H_AFTER = 6
H_FLIP = 6
Y_STEPS = (7, 8, 12, 13)
Q_START = 2
Q_EVERY = 1.0
D_LEAD = 2
G_LAG = 1
V_EXITS = ()
LOADS = ((0, 2), (2, 2), (4, 2), (6, 2), (8, 2), (10, 2), (12, 2), (14, 2))
V_H = ()
HALVES = False
EARLY = ()
OUT_LAG = 2
OUT_PER = 2
SG_UNITS = ()
Q_ALL = 40
UNITS = ((0, 2, "V", "S"), (2, 2, "V", "S"), (4, 2, "V", "S"), (6, 2, "V", "S"), (8, 2, "V", "S"), (10, 2, "V", "S"), (12, 2, "V", "S"), (14, 2, "V", "V"))
SKEW = True
X_STEPS = (6, 7, 11, 12)
ARS = True
C_LAG = 3
D_MORE = 8
SG_BANKS = ()
G_RELU = ()
WARM_FIRST = 0
WARM_EVERY = 0


def tile_gcnclassifer_pb_kernel(tc, h_gcn1, adj, gcn2_w, gcn2_b, out):
    nc = tc.nc
    with ExitStack() as ctx:
        keep = ctx.enter_context(tc.tile_pool(name="keep", bufs=1))
        stage = ctx.enter_context(tc.tile_pool(name="stage", bufs=9))
        lined = ctx.enter_context(tc.tile_pool(name="lined", bufs=6))
        junk = ctx.enter_context(tc.tile_pool(name="junk", bufs=2))
        small = ctx.enter_context(tc.tile_pool(name="small", bufs=4))
        ps_t = ctx.enter_context(tc.psum_pool(name="ps_t", bufs=7))
        ps_d = ctx.enter_context(tc.psum_pool(name="ps_d", bufs=1))

        ones = keep.tile([P, 2], BF16)
        nc.vector.memset(ones[:], 1.0)
        one = keep.tile([P, 1], F32)
        nc.vector.memset(one[:], 1.0)
        warm = keep.tile([P, 1], F32)
        nc.scalar.activation(out=warm[:], in_=one[:], func=ACT.Abs_reciprocal_sqrt if ARS else ACT.Sqrt)
        ident = keep.tile([P, P], F32)
        make_identity(nc, ident[:])

        a_sb = keep.tile([P, TILES, N_NODES], BF16)
        w_sb = keep.tile([P, 2, G_OUT], BF16)
        h_sb = keep.tile([P, TILES, H_IN], BF16)
        bias = keep.tile([P, G_OUT], BF16)

        adj_v = adj.rearrange("(b p e) j -> p b e j", p=P, e=4)
        if HALVES:
            nc.sync.dma_start(out=a_sb[:, 0, 0:HALF], in_=adj_v[:, 0, 0, 0:HALF])
            nc.sync.dma_start(out=a_sb[:, 0, HALF:N_NODES], in_=adj_v[:, 0, 0, HALF:N_NODES])
        for r, n in LOADS:
            nc.sync.dma_start(out=a_sb[:, r : r + n, :], in_=adj_v[:, r // 4, r % 4 : r % 4 + n, :])
            if r == H_AFTER:
                nc.sync.dma_start(out=w_sb[:], in_=gcn2_w.rearrange("(q k) g -> q k g", k=2))
                nc.sync.dma_start(
                    out=h_sb[:].rearrange("p (b e) k -> p b (e k)", e=4),
                    in_=h_gcn1.rearrange("(b p e) k -> p b (e k)", p=P, e=4),
                )
        nc.sync.dma_start(out=bias[:], in_=gcn2_b.partition_broadcast(P))

        deg = keep.tile([P, TILES, 8], F32)
        dis = keep.tile([P, TILES], F32)
        codes = keep.tile([P, TILES, 512], U32, align_bytes=64)
        scales = keep.tile([P, TILES, 512], U8, align_bytes=64)
        h_t = keep.tile([P, TILES, P], F32)
        y_g = keep.tile([P, PASSES, G_OUT, 4], BF16, align_bytes=64)
        y_codes = keep.tile([P, PASSES, G_OUT], U32, align_bytes=64)
        y_scales = keep.tile([P, PASSES, G_OUT], U8, align_bytes=64)
        z_sb = keep.tile([P, TILES, G_OUT], F32)
        o_sb = keep.tile([P, TILES, G_OUT], F32)
        out_v = out.rearrange("(b p e) g -> p b (e g)", p=P, e=4)
        deg_ps = ps_d.tile([P, 256, 2], F32)
        grouped = {}
        in_line = {}
        banks = {}
        acc = {}
        waiting = []

        def degree(r):
            if KINDS[r] == "V":
                row = lined.tile([P, 2, 512, 2], BF16, name="row")
                in_line[r] = row
                nc.vector.tensor_scalar(
                    out=row[:],
                    in0=a_sb[:, r, :].rearrange("p (q u e) -> p u q e", u=2, e=2),
                    scalar1=1.0,
                    scalar2=0.0,
                    op0=ALU.mult,
                    op1=ALU.add,
                    accum_out=deg[:, r, 0:1],
                )
            elif KINDS[r] == "U":
                jv = junk.tile([P, HALF], F32, name="jv")
                nc.vector.scalar_tensor_tensor(
                    out=jv[:],
                    in0=a_sb[:, r, 0:HALF],
                    scalar=1.0,
                    in1=a_sb[:, r, HALF:N_NODES],
                    op0=ALU.mult,
                    op1=ALU.add,
                    accum_out=deg[:, r, 0:1],
                )
            elif KINDS[r] == "G":
                quads = a_sb[:, r, :].rearrange("p (a b) -> p a b", a=4)
                pair = junk.tile([P, 2, 512], F32, name="pair")
                for a in range(2):
                    nc.gpsimd.tensor_tensor(
                        out=pair[:, a, :], in0=quads[:, 2 * a, :], in1=quads[:, 2 * a + 1, :], op=ALU.add
                    )
                part = junk.tile([P, 512], F32, name="part")
                nc.gpsimd.tensor_tensor(out=part[:], in0=pair[:, 0, :], in1=pair[:, 1, :], op=ALU.add)
                banks["part", r] = part
            elif KINDS[r] == "A":
                row = lined.tile([P, 2, 512, 2], BF16, name="row")
                in_line[r] = row
                nc.scalar.activation(
                    out=row[:],
                    in_=a_sb[:, r, :].rearrange("p (q u e) -> p u q e", u=2, e=2),
                    func=ACT.Copy,
                    accum_out=deg[:, r, 0:1],
                )
            elif KINDS[r] == "S":
                js = junk.tile([P, N_NODES], BF16, name="js")
                nc.scalar.activation(out=js[:], in_=a_sb[:, r, :], func=ACT.Copy, accum_out=deg[:, r, 0:1])

        def close_degree(r):
            full = junk.tile([P, 512], F32, name="full")
            nc.scalar.activation(out=full[:], in_=banks["part", r][:], func=ACT.Copy, accum_out=deg[:, r, 0:1])

        def pe_degree(r):
            by_k = grouped[r][:].rearrange("p (c i t) -> p c i t", c=4, t=4)
            for c in range(4):
                for t in range(4):
                    nc.tensor.matmul(
                        out=deg_ps[:, r, 0:1],
                        lhsT=by_k[:, c, :, t],
                        rhs=ones[:, 0:1],
                        start=(c == 0 and t == 0),
                        stop=(c == 3 and t == 3),
                    )

        def transposes(r):
            words = a_sb[:, r, :].bitcast(F32)
            for half in range(2):
                xt = ps_t.tile([P, 2, 2, P], F32, name="xt")
                banks[r, half] = xt
                for cc in range(2):
                    for u in range(2):
                        c = 2 * half + cc
                        if r in in_line:
                            src = in_line[r][:, u, 128 * c : 128 * c + 128, :].rearrange("p q e -> p (q e)").bitcast(F32)
                        else:
                            src = words[:, 256 * c + u : 256 * c + 256 : 2]
                        nc.tensor.transpose(xt[:, cc, u, :], src, ident[:])

        def exits(r):
            g_t = stage.tile([P, 4 * 512], BF16, align_bytes=64, name="g_t")
            grouped[r] = g_t
            g_w = g_t[:].bitcast(F32).rearrange("p (c i u) -> p c i u", c=4, u=2)
            for half in range(2):
                src = banks[r, half][:].rearrange("p c u i -> p c i u")
                dst = g_w[:, 2 * half : 2 * half + 2, :, :]
                if (r, half) in V_EXITS:
                    nc.vector.tensor_copy(out=dst, in_=src)
                else:
                    nc.scalar.copy(out=dst, in_=src)

        def quantise(r):
            nc.vector.quantize_mx(
                out=codes[:, r, :].bitcast(FP8X4), scales=scales[:, r, :], in_=grouped[r][:]
            )

        def flip_h():
            h_w = h_sb[:].bitcast(F32)
            for q in range(PASSES):
                ht = ps_t.tile([P, 4, P], F32, name="xt")
                for t in range(4):
                    nc.tensor.transpose(ht[:, t, :], h_w[:, 4 * q + t, :], ident[:])
                if q in V_H:
                    nc.vector.tensor_copy(out=h_t[:, 4 * q : 4 * q + 4, :], in_=ht[:])
                else:
                    nc.scalar.copy(out=h_t[:, 4 * q : 4 * q + 4, :], in_=ht[:])

        def project(c):
            h_b = h_t[:].bitcast(BF16).rearrange("p r (j k) -> p r j k", k=2)
            xw = ps_t.tile([P, 4, G_OUT], F32, name="xt")
            banks["xw", c] = xw
            for t in range(4):
                for k in range(2):
                    nc.tensor.matmul(
                        out=xw[:, t, :],
                        lhsT=h_b[:, 4 * c + t, :, k],
                        rhs=w_sb[:, k, :],
                        start=(k == 0),
                        stop=(k == 1),
                    )

        def make_dis(c):
            rt = small.tile([P, 4], F32, name="rt")
            banks["rt", c] = rt
            t0 = 0
            while t0 < 4:
                t1 = t0
                while t1 < 4 and (KINDS[4 * c + t1] == "P") == (KINDS[4 * c + t0] == "P"):
                    t1 += 1
                src = deg_ps if KINDS[4 * c + t0] == "P" else deg
                if ARS:
                    nc.scalar.activation(
                        out=dis[:, 4 * c + t0 : 4 * c + t1], in_=src[:, 4 * c + t0 : 4 * c + t1, 0], func=ACT.Abs_reciprocal_sqrt
                    )
                else:
                    nc.scalar.sqrt(out=rt[:, t0:t1], in_=src[:, 4 * c + t0 : 4 * c + t1, 0])
                t0 = t1

        def make_y(c):
            rt = banks["rt", c]
            if not ARS:
                nc.vector.reciprocal(out=dis[:, 4 * c : 4 * c + 4], in_=rt[:])
            nc.vector.tensor_tensor(
                out=y_g[:, c, :, :],
                in0=banks["xw", c][:].rearrange("p t g -> p g t"),
                in1=dis[:, 4 * c : 4 * c + 4].unsqueeze(1).to_broadcast([P, G_OUT, 4]),
                op=ALU.mult,
            )

        def quantise_y(c):
            nc.vector.quantize_mx(
                out=y_codes[:, c, :].bitcast(FP8X4),
                scales=y_scales[:, c, :],
                in_=y_g[:, c, :, :].rearrange("p g t -> p (g t)"),
            )

        def dummy():
            nc.tensor.matmul(out=deg_ps[:].rearrange("p a b -> p (a b)")[:, 384:512], lhsT=ident[:], rhs=ident[:], start=True, stop=True)

        def passes(m, ks):
            r0, n, by, relu = UNITS[m]
            if m not in acc:
                acc_ps = ps_t.tile([P, 4, G_OUT], F32, name="xt")
                acc[m] = acc_ps
            for k in ks:
                for t in range(n):
                    r = r0 + t
                    nc.tensor.matmul_mx(
                        out=acc[m][:, t, :],
                        lhsT=codes[:, r, 128 * k : 128 * k + 128].bitcast(FP8X4),
                        lhsT_scale=scales[:, r, 128 * k : 128 * k + 128],
                        rhs=y_codes[:, k, :].bitcast(FP8X4),
                        rhs_scale=y_scales[:, k, :],
                        start=(k == 0 and t == 0),
                        stop=(k == PASSES - 1 and t == n - 1),
                    )

        def scale_and_bias(r, src):
            nc.vector.scalar_tensor_tensor(
                out=z_sb[:, r, :],
                in0=src,
                scalar=dis[:, r : r + 1],
                in1=bias[:],
                op0=ALU.mult,
                op1=ALU.add,
            )

        def finish(m):
            r0, n, by, relu = UNITS[m]
            src = z_sb[:, r0 : r0 + n, :]
            dst = o_sb[:, r0 : r0 + n, :]
            if relu == "V":
                nc.vector.tensor_scalar(out=dst, in0=src, scalar1=0.0, scalar2=None, op0=ALU.max)
            elif relu == "G":
                nc.gpsimd.tensor_scalar(out=dst, in0=src, scalar1=3.0e38, scalar2=0.0, op0=ALU.min, op1=ALU.max)
            else:
                nc.scalar.activation(out=dst, in_=src, func=ACT.Relu)
            b, t0 = divmod(r0, 4)
            nc.sync.dma_start(
                out=out_v[:, b, G_OUT * t0 : G_OUT * (t0 + n)], in_=dst.rearrange("p e g -> p (e g)")
            )

        def emit_out(m):
            r0, n, by, relu = UNITS[m]
            for t in range(n):
                r = r0 + t
                if by == "S":
                    nc.scalar.activation(
                        out=z_sb[:, r, :], in_=acc[m][:, t, :], func=ACT.Copy, scale=dis[:, r : r + 1]
                    )
                else:
                    scale_and_bias(r, acc[m][:, t, :])
            if by == "S":
                nc.gpsimd.tensor_tensor(
                    out=z_sb[:, r0 : r0 + n, :],
                    in0=z_sb[:, r0 : r0 + n, :],
                    in1=bias[:].unsqueeze(1).to_broadcast([P, n, G_OUT]),
                    op=ALU.add,
                )
                if relu == "G":
                    finish(m)
                else:
                    waiting.append(m)
            else:
                while waiting:
                    finish(waiting.pop(0))
                finish(m)

        with tc.manual_schedule():
            nq = 0
            nlead = 1
            done = 0
            for s in range(TILES + 16):
                if s in Y_STEPS:
                    make_dis(Y_STEPS.index(s))
                if s < TILES:
                    if s == 0:
                        degree(0)
                    transposes(s)
                if 0 <= s - G_LAG < TILES and KINDS[s - G_LAG] == "P":
                    pe_degree(s - G_LAG)
                if s < TILES:
                    exits(s)
                while nlead < TILES and nlead <= s + D_LEAD + (s >= D_MORE):
                    degree(nlead)
                    nlead += 1
                if s >= C_LAG and s - C_LAG < TILES and KINDS[s - C_LAG] == "G":
                    close_degree(s - C_LAG)
                if s == H_FLIP:
                    flip_h()
                if s in X_STEPS:
                    project(X_STEPS.index(s))
                if s in Y_STEPS:
                    make_y(Y_STEPS.index(s))
                while nq < TILES and (Q_START + Q_EVERY * nq <= s or s >= Q_ALL):
                    quantise(nq)
                    nq += 1
                if s in Y_STEPS:
                    quantise_y(Y_STEPS.index(s))
                for m in range(len(EARLY)):
                    if s == EARLY[m]:
                        passes(m, range(3))
                if s >= Y_STEPS[3] + OUT_LAG:
                    for i in range(OUT_PER):
                        if done < len(UNITS) and nq >= UNITS[done][0] + UNITS[done][1]:
                            passes(done, range(3, 4) if done < len(EARLY) else range(4))
                            if done > 0:
                                emit_out(done - 1)
                            done += 1
                            if done == len(UNITS):
                                emit_out(done - 1)
            for m in waiting:
                finish(m)
            assert done == len(UNITS) and nq == TILES and nlead == TILES
